import numpy as np
import ml_dtypes


def mxq(x, axis, fmt="e4m3"):
    dtype, down = {"e4m3": (ml_dtypes.float8_e4m3fn, 7), "e5m2": (ml_dtypes.float8_e5m2, 14)}[fmt]
    v = np.moveaxis(np.asarray(x, np.float32).astype(ml_dtypes.bfloat16).astype(np.float64), axis, -1)
    blocks = v.reshape(v.shape[:-1] + (-1, 32))
    amax = np.abs(blocks).max(-1, keepdims=True)
    byte = np.maximum(np.where(amax > 0, np.frexp(amax)[1] - 1 + 127, 0) - down, 1)
    scale = np.exp2(byte - 127.0)
    codes = (blocks / scale).astype(np.float32).astype(dtype).astype(np.float64)
    return np.moveaxis((codes * scale).reshape(v.shape), -1, axis)


WIDE = False


def mx_kscale(k):
    if not WIDE:
        return np.ones(k)
    levels = np.array([30, -30])
    if k % 512:
        return np.exp2(np.random.permutation(np.resize(levels, k // 32))).repeat(32)
    a = np.empty((k // 512, 16))
    for p in range(k // 512):
        a[p, :8] = np.random.permutation(np.resize(levels, 8))
        for g in range(8):
            far = levels[np.abs(levels - a[p, g]) >= 10]
            a[p, g + 8] = far[np.random.randint(len(far))]
    return np.exp2(a.ravel()).repeat(32)


BF16 = ml_dtypes.bfloat16


def bf(x):
    return np.asarray(x, np.float32).astype(BF16)


def f64(x):
    return np.asarray(x).astype(np.float64)


E2M1 = np.array([0.0, 0.5, 1.0, 1.5, 2.0, 3.0, 4.0, 6.0, -0.0, -0.5, -1.0, -1.5, -2.0, -3.0, -4.0, -6.0])


def pack_weight(w, fmt):
    k, n = w.shape
    w = f64(bf(w)).reshape(k // 32, 32, n)
    amax = np.abs(w).max(1)
    if fmt == "e4m3":
        byte = np.frexp(amax)[1] - 1 + 127 - 7
    else:
        mant, ex = np.frexp(amax / 6.0)
        byte = np.where(mant > 0.5, ex, ex - 1) + 127
    byte = np.clip(np.where(amax > 0, byte, 1), 1, 254)
    scaled = (w * np.exp2(127.0 - byte)[:, None, :]).reshape(k, n).astype(np.float32)
    by_word = np.ascontiguousarray(scaled.reshape(k // 512, 128, 4, n).transpose(0, 1, 3, 2))
    if fmt == "e4m3":
        words = by_word.astype(ml_dtypes.float8_e4m3fn).view(np.uint8)
    else:
        c = by_word.astype(ml_dtypes.float4_e2m1fn).view(np.uint8) & 0xF
        words = c[..., 0::2] | (c[..., 1::2] << 4)
    return np.ascontiguousarray(words), np.ascontiguousarray(byte.astype(np.uint8).reshape(k // 512, 16, n))


def unpack_weight(words, scales, fmt):
    g, p, n, _ = words.shape
    if fmt == "e4m3":
        vals = np.ascontiguousarray(words).view(ml_dtypes.float8_e4m3fn).astype(np.float64)
    else:
        nib = np.empty((g, p, n, 4), np.uint8)
        nib[..., 0::2] = words & 0xF
        nib[..., 1::2] = words >> 4
        vals = E2M1[nib]
    vals = vals * np.repeat(np.exp2(scales.astype(np.float64) - 127.0), 8, axis=1)[..., None]
    return vals.transpose(0, 1, 3, 2).reshape(g * 512, n)

def pack4(w):
    words, scales = pack_weight(w, "e2m1")
    return words.reshape(words.shape[0], 128, -1), scales


def unpack4(words, scales):
    return unpack_weight(words.reshape(words.shape[0], 128, -1, 2), scales, "e2m1")


B, C, H, W = 1, 512, 64, 32
CH = C // 2
N = H * W
QS = 1.35 * CH ** -0.25


def pool2(t):
    r = t.reshape(B, -1, H // 2, 2, W // 2, 2)
    return r.max(axis=(3, 5)) + r.mean(axis=(3, 5))


def setup_inputs():
    s = mx_kscale(C)
    x = bf(np.random.standard_normal((B, C, H, W)) * s[None, :, None, None])
    w1 = np.random.standard_normal((CH, C)) * QS / np.sqrt(C) / s
    w2 = np.random.standard_normal((CH, C)) * QS / np.sqrt(C) / s
    W1_words, W1_scales = pack4(np.ascontiguousarray(w1.T))
    W2_words, W2_scales = pack4(np.ascontiguousarray(w2.T))
    return {"x": x,
            "W1_words": W1_words, "W1_scales": W1_scales,
            "W2_words": W2_words, "W2_scales": W2_scales}


def reference(x, W1_words, W1_scales, W2_words, W2_scales):
    xq = mxq(f64(x).reshape(B, C, N), 1, "e5m2")
    c1 = unpack4(W1_words, W1_scales).T @ xq
    c2 = unpack4(W2_words, W2_scales).T @ xq
    return pool2(c1.reshape(B, CH, H, W)), c2.reshape(B, CH, H, W)

@@ -1,0 +1,183 @@
+from contextlib import ExitStack
+
+import concourse.mybir as mybir
+
+C, CH, H, W = 512, 256, 64, 32
+NPIX = H * W
+FLOPS = 2 * 2 * CH * C * NPIX
+
+F32 = mybir.dt.float32
+BF16 = mybir.dt.bfloat16
+I32 = mybir.dt.int32
+U32 = mybir.dt.uint32
+U8 = mybir.dt.uint8
+E5M2X4 = mybir.dt.float8_e5m2_x4
+E2M1X4 = mybir.dt.float4_e2m1fn_x4
+ALU = mybir.AluOpType
+
+P = 128
+PACK = 4
+CHUNK = 512
+NCHUNK = NPIX // CHUNK
+WROWS = 8
+WIN = CHUNK // 4
+HALVES = CH // P
+
+VEC_ROWS = {0: (4, 0), 1: (8, 0), 2: (8, 0), 3: (6, 0)}
+
+
+def tile_selfspatialattentionmodule_pa_kernel(
+    tc, x, W1_words, W1_scales, W2_words, W2_scales, out_0, out_1
+):
+    nc = tc.nc
+    xk = x[0].rearrange("(p t) h w -> p t (h w)", t=PACK)
+    pooled_hbm = out_0[0].rearrange("(g p) i j -> p g (i j)", p=P)
+    c2_hbm = out_1[0].rearrange("c h w -> c (h w)")
+
+    with ExitStack() as ctx:
+        keep = ctx.enter_context(tc.tile_pool(name="keep", bufs=1))
+        psum = ctx.enter_context(tc.psum_pool(name="psum", bufs=1))
+        ctx.enter_context(tc.manual_schedule())
+
+        words = [keep.tile([P, 2 * CH], U8, name="words%d" % m, align_bytes=64) for m in range(2)]
+        planes = [keep.tile([P, CH], U8, name="plane%d" % m, align_bytes=64) for m in range(2)]
+        for m in (1, 0):
+            nc.vector.memset(planes[m][:].bitcast(I32), 0)
+
+        def load_weight(eng, m, w_words, w_scales):
+            eng.dma_start(out=words[m][:].bitcast(I32), in_=w_words[0].bitcast(I32))
+            for q in range(4):
+                eng.dma_start(
+                    out=planes[m][32 * q : 32 * q + 4, :].bitcast(I32),
+                    in_=w_scales[0, 4 * q : 4 * q + 4, :].bitcast(I32),
+                )
+
+        pieces = {}
+
+        def load_x(c, r0, r1):
+            raw = keep.tile([P, PACK, 64 * (r1 - r0)], BF16, name="raw%d_%d" % (c, r0), align_bytes=64)
+            nc.sync.dma_start(out=raw[:], in_=xk[:, :, c * CHUNK + 64 * r0 : c * CHUNK + 64 * r1])
+            pieces.setdefault(c, []).append((raw, r0, r1))
+
+        load_weight(nc.scalar, 1, W2_words, W2_scales)
+        load_x(0, 0, 4)
+        load_x(0, 4, 8)
+        load_x(1, 0, 8)
+        load_weight(nc.sync, 0, W1_words, W1_scales)
+        load_x(2, 0, 8)
+        load_x(3, 0, 8)
+
+        grouped = [keep.tile([P, PACK * CHUNK], BF16, name="grouped%d" % c, align_bytes=64) for c in range(NCHUNK)]
+        codes = [keep.tile([P, CHUNK], U32, name="codes%d" % c, align_bytes=64) for c in range(NCHUNK)]
+        scales = [keep.tile([P, CHUNK], U8, name="scales%d" % c, align_bytes=64) for c in range(NCHUNK)]
+        maxes = [keep.tile([P, HALVES * WIN], F32, name="maxes%d" % c) for c in range(NCHUNK)]
+        c1_bank = {}
+        c2_bank = {}
+        sum_bank = {}
+
+        def interleave(on_vector, c, piece, a):
+            raw, r0, r1 = pieces[c][piece]
+            n = VEC_ROWS[c][a]
+            lo, hi = (0, n) if on_vector else (n, r1 - r0)
+            if lo == hi:
+                return
+            src = raw[:].rearrange("p t (i a jc j2 b) -> p a i jc t j2 b", a=2, jc=8, j2=2, b=2)[:, a, lo:hi]
+            dst = grouped[c][:].rearrange("p (a b i jc j2 t) -> p a i jc t j2 b", a=2, b=2, i=WROWS, jc=8, j2=2)[
+                :, a, r0 + lo : r0 + hi
+            ]
+            if on_vector:
+                nc.vector.tensor_copy(out=dst, in_=src)
+            else:
+                nc.scalar.copy(out=dst, in_=src)
+
+        def quantize(c, lo, hi):
+            nc.vector.quantize_mx(
+                out=codes[c][:, lo:hi].bitcast(E5M2X4),
+                scales=scales[c][:, lo:hi],
+                in_=grouped[c][:, PACK * lo : PACK * hi],
+            )
+
+        def mx(out, m, g, c, lo, hi, start, stop):
+            nc.tensor.matmul_mx(
+                out=out,
+                lhsT=words[m][:, 2 * P * g : 2 * P * (g + 1)].bitcast(E2M1X4),
+                lhsT_scale=planes[m][:, P * g : P * (g + 1)],
+                rhs=codes[c][:, lo:hi].bitcast(E5M2X4),
+                rhs_scale=scales[c][:, lo:hi],
+                start=start,
+                stop=stop,
+            )
+
+        def product(m, c, g):
+            banks = c2_bank if m else c1_bank
+            banks[c, g] = psum.tile([P, CHUNK], F32, name="bank%d_%d" % (m, (c * HALVES + g) % 3))
+            mx(banks[c, g][:], m, g, c, 0, CHUNK, True, True)
+
+        def window_sums(c):
+            sum_bank[c] = psum.tile([P, HALVES * WIN], F32, name="sum_bank%d" % (c % 2))
+            for g in range(HALVES):
+                for pos in range(4):
+                    mx(sum_bank[c][:, g * WIN : (g + 1) * WIN], 0, g, c, pos * WIN, (pos + 1) * WIN, pos == 0, pos == 3)
+
+        def c2_out(c, g):
+            stage = keep.tile([P, CHUNK], F32, name="c2_stage%d_%d" % (c, g))
+            nc.scalar.copy(
+                out=stage[:].rearrange("p (i a j b) -> p i a j b", a=2, j=16, b=2),
+                in_=c2_bank[c, g][:].rearrange("p (a b i j) -> p i a j b", a=2, b=2, j=16),
+            )
+            nc.sync.dma_start(out=c2_hbm[g * P : (g + 1) * P, c * CHUNK : (c + 1) * CHUNK], in_=stage[:])
+
+        def window_max(c, g):
+            nc.vector.tensor_reduce(
+                out=maxes[c][:, g * WIN : (g + 1) * WIN],
+                in_=c1_bank[c, g][:].rearrange("p (pos w) -> p w pos", pos=4),
+                axis=mybir.AxisListType.X,
+                op=ALU.max,
+            )
+
+        def pooled_out(c):
+            stage = keep.tile([P, HALVES * WIN], F32, name="pooled%d" % c)
+            nc.vector.scalar_tensor_tensor(
+                out=stage[:], in0=sum_bank[c][:], scalar=0.25, in1=maxes[c][:], op0=ALU.mult, op1=ALU.add
+            )
+            nc.sync.dma_start(
+                out=pooled_hbm[:, :, c * WIN : (c + 1) * WIN], in_=stage[:].rearrange("p (g w) -> p g w", g=HALVES)
+            )
+
+        def interleave_chunk(c):
+            for piece in range(len(pieces[c])):
+                for a in range(2):
+                    interleave(True, c, piece, a)
+                    interleave(False, c, piece, a)
+
+        def quantize_chunk(c):
+            quantize(c, 0, CHUNK // 2)
+            quantize(c, CHUNK // 2, CHUNK)
+
+        interleave_chunk(0)
+        quantize_chunk(0)
+        product(1, 0, 0)
+        product(0, 0, 0)
+        product(0, 0, 1)
+        product(1, 0, 1)
+        window_sums(0)
+        interleave_chunk(1)
+        quantize_chunk(1)
+        for c in range(NCHUNK):
+            more = c + 1 < NCHUNK
+            if more:
+                product(0, c + 1, 0)
+                product(1, c + 1, 0)
+            window_max(c, 0)
+            c2_out(c, 0)
+            if c + 2 < NCHUNK:
+                interleave_chunk(c + 2)
+            window_max(c, 1)
+            c2_out(c, 1)
+            if c + 2 < NCHUNK:
+                quantize_chunk(c + 2)
+            if more:
+                product(0, c + 1, 1)
+                product(1, c + 1, 1)
+                window_sums(c + 1)
+            pooled_out(c)

@@ -23,7 +23,7 @@ WROWS = 8
 WIN = CHUNK // 4
 HALVES = CH // P
 
-VEC_ROWS = {0: (4, 0), 1: (8, 0), 2: (8, 0), 3: (6, 0)}
+VEC_ROWS = {(0, 0): (4, 4), (0, 1): (4, 0), (1, 0): (8, 2), (2, 0): (8, 0), (3, 0): (6, 0)}
 
 
 def tile_selfspatialattentionmodule_pa_kernel(
@@ -77,7 +77,7 @@ def tile_selfspatialattentionmodule_pa_kernel(
 
         def interleave(on_vector, c, piece, a):
             raw, r0, r1 = pieces[c][piece]
-            n = VEC_ROWS[c][a]
+            n = VEC_ROWS[c, piece][a]
             lo, hi = (0, n) if on_vector else (n, r1 - r0)
             if lo == hi:
                 return
@@ -135,13 +135,14 @@ def tile_selfspatialattentionmodule_pa_kernel(
                 op=ALU.max,
             )
 
-        def pooled_out(c):
-            stage = keep.tile([P, HALVES * WIN], F32, name="pooled%d" % c)
+        def pooled_out(c, g0, g1):
+            cols = slice(g0 * WIN, g1 * WIN)
+            stage = keep.tile([P, (g1 - g0) * WIN], F32, name="pooled%d_%d" % (c, g0))
             nc.vector.scalar_tensor_tensor(
-                out=stage[:], in0=sum_bank[c][:], scalar=0.25, in1=maxes[c][:], op0=ALU.mult, op1=ALU.add
+                out=stage[:], in0=sum_bank[c][:, cols], scalar=0.25, in1=maxes[c][:, cols], op0=ALU.mult, op1=ALU.add
             )
             nc.sync.dma_start(
-                out=pooled_hbm[:, :, c * WIN : (c + 1) * WIN], in_=stage[:].rearrange("p (g w) -> p g w", g=HALVES)
+                out=pooled_hbm[:, g0:g1, c * WIN : (c + 1) * WIN], in_=stage[:].rearrange("p (g w) -> p g w", w=WIN)
             )
 
         def interleave_chunk(c):
@@ -163,21 +164,32 @@ def tile_selfspatialattentionmodule_pa_kernel(
         window_sums(0)
         interleave_chunk(1)
         quantize_chunk(1)
-        for c in range(NCHUNK):
-            more = c + 1 < NCHUNK
-            if more:
-                product(0, c + 1, 0)
-                product(1, c + 1, 0)
+        for c in range(NCHUNK - 2):
+            product(0, c + 1, 0)
+            product(1, c + 1, 0)
             window_max(c, 0)
             c2_out(c, 0)
-            if c + 2 < NCHUNK:
-                interleave_chunk(c + 2)
+            interleave_chunk(c + 2)
             window_max(c, 1)
             c2_out(c, 1)
-            if c + 2 < NCHUNK:
-                quantize_chunk(c + 2)
-            if more:
-                product(0, c + 1, 1)
-                product(1, c + 1, 1)
-                window_sums(c + 1)
-            pooled_out(c)
+            quantize_chunk(c + 2)
+            product(0, c + 1, 1)
+            product(1, c + 1, 1)
+            window_sums(c + 1)
+            pooled_out(c, 0, HALVES)
+        c, last = NCHUNK - 2, NCHUNK - 1
+        product(0, last, 0)
+        product(1, last, 0)
+        for g in range(HALVES):
+            window_max(c, g)
+            c2_out(c, g)
+        product(0, last, 1)
+        product(1, last, 1)
+        window_sums(last)
+        window_max(last, 0)
+        c2_out(last, 0)
+        pooled_out(c, 0, HALVES)
+        window_max(last, 1)
+        c2_out(last, 1)
+        for g in range(HALVES):
+            pooled_out(last, g, g + 1)

from contextlib import ExitStack

import concourse.mybir as mybir

C, CH, H, W = 512, 256, 64, 32
NPIX = H * W
FLOPS = 2 * 2 * CH * C * NPIX

F32 = mybir.dt.float32
BF16 = mybir.dt.bfloat16
I32 = mybir.dt.int32
U32 = mybir.dt.uint32
U8 = mybir.dt.uint8
E5M2X4 = mybir.dt.float8_e5m2_x4
E2M1X4 = mybir.dt.float4_e2m1fn_x4
ALU = mybir.AluOpType

P = 128
PACK = 4
CHUNK = 512
NCHUNK = NPIX // CHUNK
WROWS = 8
WIN = CHUNK // 4
HALVES = CH // P

VEC_ROWS = {(0, 0): (4, 4), (0, 1): (4, 0), (1, 0): (8, 2), (2, 0): (8, 0), (3, 0): (6, 0)}


def tile_selfspatialattentionmodule_pa_kernel(
    tc, x, W1_words, W1_scales, W2_words, W2_scales, out_0, out_1
):
    nc = tc.nc
    xk = x[0].rearrange("(p t) h w -> p t (h w)", t=PACK)
    pooled_hbm = out_0[0].rearrange("(g p) i j -> p g (i j)", p=P)
    c2_hbm = out_1[0].rearrange("c h w -> c (h w)")

    with ExitStack() as ctx:
        keep = ctx.enter_context(tc.tile_pool(name="keep", bufs=1))
        psum = ctx.enter_context(tc.psum_pool(name="psum", bufs=1))
        ctx.enter_context(tc.manual_schedule())

        words = [keep.tile([P, 2 * CH], U8, name="words%d" % m, align_bytes=64) for m in range(2)]
        planes = [keep.tile([P, CH], U8, name="plane%d" % m, align_bytes=64) for m in range(2)]
        for m in (1, 0):
            nc.vector.memset(planes[m][:].bitcast(I32), 0)

        def load_weight(eng, m, w_words, w_scales):
            eng.dma_start(out=words[m][:].bitcast(I32), in_=w_words[0].bitcast(I32))
            for q in range(4):
                eng.dma_start(
                    out=planes[m][32 * q : 32 * q + 4, :].bitcast(I32),
                    in_=w_scales[0, 4 * q : 4 * q + 4, :].bitcast(I32),
                )

        pieces = {}

        def load_x(c, r0, r1):
            raw = keep.tile([P, PACK, 64 * (r1 - r0)], BF16, name="raw%d_%d" % (c, r0), align_bytes=64)
            nc.sync.dma_start(out=raw[:], in_=xk[:, :, c * CHUNK + 64 * r0 : c * CHUNK + 64 * r1])
            pieces.setdefault(c, []).append((raw, r0, r1))

        load_weight(nc.scalar, 1, W2_words, W2_scales)
        load_x(0, 0, 4)
        load_x(0, 4, 8)
        load_x(1, 0, 8)
        load_weight(nc.sync, 0, W1_words, W1_scales)
        load_x(2, 0, 8)
        load_x(3, 0, 8)

        grouped = [keep.tile([P, PACK * CHUNK], BF16, name="grouped%d" % c, align_bytes=64) for c in range(NCHUNK)]
        codes = [keep.tile([P, CHUNK], U32, name="codes%d" % c, align_bytes=64) for c in range(NCHUNK)]
        scales = [keep.tile([P, CHUNK], U8, name="scales%d" % c, align_bytes=64) for c in range(NCHUNK)]
        maxes = [keep.tile([P, HALVES * WIN], F32, name="maxes%d" % c) for c in range(NCHUNK)]
        c1_bank = {}
        c2_bank = {}
        sum_bank = {}

        def interleave(on_vector, c, piece, a):
            raw, r0, r1 = pieces[c][piece]
            n = VEC_ROWS[c, piece][a]
            lo, hi = (0, n) if on_vector else (n, r1 - r0)
            if lo == hi:
                return
            src = raw[:].rearrange("p t (i a jc j2 b) -> p a i jc t j2 b", a=2, jc=8, j2=2, b=2)[:, a, lo:hi]
            dst = grouped[c][:].rearrange("p (a b i jc j2 t) -> p a i jc t j2 b", a=2, b=2, i=WROWS, jc=8, j2=2)[
                :, a, r0 + lo : r0 + hi
            ]
            if on_vector:
                nc.vector.tensor_copy(out=dst, in_=src)
            else:
                nc.scalar.copy(out=dst, in_=src)

        def quantize(c, lo, hi):
            nc.vector.quantize_mx(
                out=codes[c][:, lo:hi].bitcast(E5M2X4),
                scales=scales[c][:, lo:hi],
                in_=grouped[c][:, PACK * lo : PACK * hi],
            )

        def mx(out, m, g, c, lo, hi, start, stop):
            nc.tensor.matmul_mx(
                out=out,
                lhsT=words[m][:, 2 * P * g : 2 * P * (g + 1)].bitcast(E2M1X4),
                lhsT_scale=planes[m][:, P * g : P * (g + 1)],
                rhs=codes[c][:, lo:hi].bitcast(E5M2X4),
                rhs_scale=scales[c][:, lo:hi],
                start=start,
                stop=stop,
            )

        def product(m, c, g):
            banks = c2_bank if m else c1_bank
            banks[c, g] = psum.tile([P, CHUNK], F32, name="bank%d_%d" % (m, (c * HALVES + g) % 3))
            mx(banks[c, g][:], m, g, c, 0, CHUNK, True, True)

        def window_sums(c):
            sum_bank[c] = psum.tile([P, HALVES * WIN], F32, name="sum_bank%d" % (c % 2))
            for g in range(HALVES):
                for pos in range(4):
                    mx(sum_bank[c][:, g * WIN : (g + 1) * WIN], 0, g, c, pos * WIN, (pos + 1) * WIN, pos == 0, pos == 3)

        def c2_out(c, g):
            stage = keep.tile([P, CHUNK], F32, name="c2_stage%d_%d" % (c, g))
            nc.scalar.copy(
                out=stage[:].rearrange("p (i a j b) -> p i a j b", a=2, j=16, b=2),
                in_=c2_bank[c, g][:].rearrange("p (a b i j) -> p i a j b", a=2, b=2, j=16),
            )
            nc.sync.dma_start(out=c2_hbm[g * P : (g + 1) * P, c * CHUNK : (c + 1) * CHUNK], in_=stage[:])

        def window_max(c, g):
            nc.vector.tensor_reduce(
                out=maxes[c][:, g * WIN : (g + 1) * WIN],
                in_=c1_bank[c, g][:].rearrange("p (pos w) -> p w pos", pos=4),
                axis=mybir.AxisListType.X,
                op=ALU.max,
            )

        def pooled_out(c, g0, g1):
            cols = slice(g0 * WIN, g1 * WIN)
            stage = keep.tile([P, (g1 - g0) * WIN], F32, name="pooled%d_%d" % (c, g0))
            nc.vector.scalar_tensor_tensor(
                out=stage[:], in0=sum_bank[c][:, cols], scalar=0.25, in1=maxes[c][:, cols], op0=ALU.mult, op1=ALU.add
            )
            nc.sync.dma_start(
                out=pooled_hbm[:, g0:g1, c * WIN : (c + 1) * WIN], in_=stage[:].rearrange("p (g w) -> p g w", w=WIN)
            )

        def interleave_chunk(c):
            for piece in range(len(pieces[c])):
                for a in range(2):
                    interleave(True, c, piece, a)
                    interleave(False, c, piece, a)

        def quantize_chunk(c):
            quantize(c, 0, CHUNK // 2)
            quantize(c, CHUNK // 2, CHUNK)

        interleave_chunk(0)
        quantize_chunk(0)
        product(1, 0, 0)
        product(0, 0, 0)
        product(0, 0, 1)
        product(1, 0, 1)
        window_sums(0)
        interleave_chunk(1)
        quantize_chunk(1)
        for c in range(NCHUNK - 2):
            product(0, c + 1, 0)
            product(1, c + 1, 0)
            window_max(c, 0)
            c2_out(c, 0)
            interleave_chunk(c + 2)
            window_max(c, 1)
            c2_out(c, 1)
            quantize_chunk(c + 2)
            product(0, c + 1, 1)
            product(1, c + 1, 1)
            window_sums(c + 1)
            pooled_out(c, 0, HALVES)
        c, last = NCHUNK - 2, NCHUNK - 1
        product(0, last, 0)
        product(1, last, 0)
        for g in range(HALVES):
            window_max(c, g)
            c2_out(c, g)
        product(0, last, 1)
        product(1, last, 1)
        window_sums(last)
        window_max(last, 0)
        c2_out(last, 0)
        pooled_out(c, 0, HALVES)
        window_max(last, 1)
        c2_out(last, 1)
        for g in range(HALVES):
            pooled_out(last, g, g + 1)
